import numpy as np
import ml_dtypes


def mxq(x, axis, fmt="e4m3"):
    dtype, down = {"e4m3": (ml_dtypes.float8_e4m3fn, 7), "e5m2": (ml_dtypes.float8_e5m2, 14)}[fmt]
    v = np.moveaxis(np.asarray(x, np.float32).astype(ml_dtypes.bfloat16).astype(np.float64), axis, -1)
    blocks = v.reshape(v.shape[:-1] + (-1, 32))
    amax = np.abs(blocks).max(-1, keepdims=True)
    byte = np.maximum(np.where(amax > 0, np.frexp(amax)[1] - 1 + 127, 0) - down, 1)
    scale = np.exp2(byte - 127.0)
    codes = (blocks / scale).astype(np.float32).astype(dtype).astype(np.float64)
    return np.moveaxis((codes * scale).reshape(v.shape), -1, axis)


WIDE = False


def mx_kscale(k):
    if not WIDE:
        return np.ones(k)
    levels = np.array([10, -10, 5, -5, 0])
    a = np.random.permutation(np.resize(levels, k // 512 * 4)).reshape(k // 512, 4)
    idx = np.arange(k)
    return np.exp2(a[idx // 512, idx % 128 // 32])


BF16 = ml_dtypes.bfloat16


def bf(x):
    return np.asarray(x, np.float32).astype(BF16)


def f64(x):
    return np.asarray(x).astype(np.float64)


E2M1 = np.array([0.0, 0.5, 1.0, 1.5, 2.0, 3.0, 4.0, 6.0, -0.0, -0.5, -1.0, -1.5, -2.0, -3.0, -4.0, -6.0])


def pack_weight(w, fmt):
    k, n = w.shape
    w = f64(bf(w)).reshape(k // 32, 32, n)
    amax = np.abs(w).max(1)
    if fmt == "e4m3":
        byte = np.frexp(amax)[1] - 1 + 127 - 7
    else:
        mant, ex = np.frexp(amax / 6.0)
        byte = np.where(mant > 0.5, ex, ex - 1) + 127
    byte = np.clip(np.where(amax > 0, byte, 1), 1, 254)
    scaled = (w * np.exp2(127.0 - byte)[:, None, :]).reshape(k, n).astype(np.float32)
    by_word = np.ascontiguousarray(scaled.reshape(k // 512, 128, 4, n).transpose(0, 1, 3, 2))
    if fmt == "e4m3":
        words = by_word.astype(ml_dtypes.float8_e4m3fn).view(np.uint8)
    else:
        c = by_word.astype(ml_dtypes.float4_e2m1fn).view(np.uint8) & 0xF
        words = c[..., 0::2] | (c[..., 1::2] << 4)
    return np.ascontiguousarray(words), np.ascontiguousarray(byte.astype(np.uint8).reshape(k // 512, 16, n))


def unpack_weight(words, scales, fmt):
    g, p, n, _ = words.shape
    if fmt == "e4m3":
        vals = np.ascontiguousarray(words).view(ml_dtypes.float8_e4m3fn).astype(np.float64)
    else:
        nib = np.empty((g, p, n, 4), np.uint8)
        nib[..., 0::2] = words & 0xF
        nib[..., 1::2] = words >> 4
        vals = E2M1[nib]
    vals = vals * np.repeat(np.exp2(scales.astype(np.float64) - 127.0), 8, axis=1)[..., None]
    return vals.transpose(0, 1, 3, 2).reshape(g * 512, n)

def pack4(w):
    words, scales = pack_weight(w, "e2m1")
    return words.reshape(words.shape[0], 128, -1), scales


def unpack4(words, scales):
    return unpack_weight(words.reshape(words.shape[0], 128, -1, 2), scales, "e2m1")


B, T, HP, WP, NH, D, DFF = 16, 8, 3, 4, 16, 1024, 4096
HW = HP * WP


def setup_inputs():
    s = mx_kscale(D)
    c = np.random.standard_normal((B * T, 1 + HW, D)) * 1.5 / np.sqrt(1 + HW)
    c[:, 0, :] *= 5.0
    ctx_s = bf(c * s)
    x_res = bf(np.random.standard_normal((B, 1 + HW * T, D)) * 1.1)
    words, scales = pack4(np.random.standard_normal((D, D)) / np.sqrt(D) / s[:, None])
    return {"ctx_s": ctx_s,
            "x_res": x_res,
            "s_out_w_words": words,
            "s_out_w_scales": scales,
            "s_out_b": bf(0.1 * np.random.standard_normal(D))}


def reference(ctx_s, x_res, s_out_w_words, s_out_w_scales, s_out_b):
    res_s = (mxq(f64(ctx_s), 2, "e4m3") @ unpack4(s_out_w_words, s_out_w_scales)) + f64(s_out_b)
    cls_tok = res_s[:, 0, :].reshape(B, T, D).mean(axis=1, keepdims=True)
    res_p = res_s[:, 1:, :].reshape(B, T, HW, D).swapaxes(1, 2).reshape(B, HW * T, D)
    return f64(x_res) + np.concatenate([cls_tok, res_p], axis=1)

@@ -1,0 +1,237 @@
+from contextlib import ExitStack
+
+import concourse.mybir as mybir
+from concourse.masks import make_identity
+
+F32 = mybir.dt.float32
+BF16 = mybir.dt.bfloat16
+I32 = mybir.dt.int32
+U32 = mybir.dt.uint32
+U8 = mybir.dt.uint8
+FP8X4 = mybir.dt.float8_e4m3fn_x4
+FP4X4 = mybir.dt.float4_e2m1fn_x4
+ADD = mybir.AluOpType.add
+MULT = mybir.AluOpType.mult
+
+P = 128
+SAMPLES = 16
+FRAMES = 8
+PATCHES = 12
+TILES = 1 + PATCHES
+D = 1024
+K_PASS = 4 * P
+PASSES = D // K_PASS
+PAIRS = 2
+BANK = 512
+HALVES = D // BANK
+CHUNKS = D // P
+CHUNKS_A_BANK = BANK // P
+ROUND = 2
+VECTOR_EVERY = 3
+
+FLOPS = 2 * TILES * P * D * D
+
+
+def tile_timesformerlayer_pc_kernel(
+    tc, ctx_s, x_res, s_out_w_words, s_out_w_scales, s_out_b, out
+):
+    nc = tc.nc
+    with ExitStack() as stack:
+        keep = stack.enter_context(tc.tile_pool(name="keep", bufs=1))
+        ring = stack.enter_context(tc.tile_pool(name="ring", bufs=2 * ROUND))
+        turned_banks = stack.enter_context(tc.psum_pool(name="turned_banks", bufs=ROUND))
+        product_banks = stack.enter_context(tc.psum_pool(name="product_banks", bufs=ROUND * HALVES))
+        bias_banks = stack.enter_context(tc.psum_pool(name="bias_banks", bufs=1))
+        stack.enter_context(tc.manual_schedule())
+
+        w_scales = keep.tile([P, PASSES, D], U8, name="w_scales", align_bytes=64)
+        nc.vector.memset(w_scales[:].rearrange("p g n -> p (g n)").bitcast(I32), 0)
+        identity_bf = keep.tile([P, P], BF16, name="identity_bf")
+        make_identity(nc, identity_bf[:])
+        identity = keep.tile([P, P], F32, name="identity")
+        make_identity(nc, identity[:])
+
+        class_bias = keep.tile([P, P], BF16, name="class_bias")
+        nc.scalar.dma_start(
+            out=class_bias[:],
+            in_=s_out_b.rearrange("(c n) -> c n", c=CHUNKS).unsqueeze(1).to_broadcast([CHUNKS, SAMPLES, P]),
+        )
+        class_residual = keep.tile([P, P], BF16, name="class_residual")
+        nc.scalar.dma_start(
+            out=class_residual[:], in_=x_res[:, 0, :].rearrange("b (c n) -> c b n", c=CHUNKS)
+        )
+
+        tokens = []
+        class_tokens = keep.tile([P, D], BF16, name="class_tokens")
+        nc.sync.dma_start(out=class_tokens[:], in_=ctx_s[:, 0, :])
+        tokens.append(class_tokens[:])
+
+        def load_tokens(first):
+            both = keep.tile([P, ROUND, D], BF16, name="tokens%d" % first)
+            nc.sync.dma_start(out=both[:], in_=ctx_s[:, first : first + ROUND, :])
+            for i in range(ROUND):
+                tokens.append(both[:, i, :])
+
+        def rows_of_patch(tensor, p):
+            return tensor[:, 1 + p * FRAMES : 1 + (p + 1) * FRAMES, :]
+
+        load_tokens(1)
+        w_words = keep.tile([P, PASSES, 2 * D], U8, name="w_words", align_bytes=64)
+        nc.sync.dma_start(
+            out=w_words[:].bitcast(I32), in_=s_out_w_words.rearrange("g p n -> p g n").bitcast(I32)
+        )
+        for quadrant in range(4):
+            nc.sync.dma_start(
+                out=w_scales[32 * quadrant : 32 * quadrant + 4, :, :].bitcast(I32),
+                in_=s_out_w_scales[:, 4 * quadrant : 4 * quadrant + 4, :]
+                .rearrange("g r n -> r g n")
+                .bitcast(I32),
+            )
+        residual = []
+        for first in range(1, TILES, ROUND):
+            if first + ROUND < TILES:
+                load_tokens(first + ROUND)
+            for p in range(first - 1, first - 1 + ROUND):
+                rows = keep.tile([P, D], BF16, name="residual%d" % p)
+                nc.sync.dma_start(out=rows[:], in_=rows_of_patch(x_res, p))
+                residual.append(rows)
+        bias_bank = []
+        bias_sb = keep.tile([P, D], F32, name="bias_sb")
+        for h in range(HALVES):
+            bank = bias_banks.tile([P, BANK], F32, name="bias_bank%d" % h)
+            for i in range(CHUNKS_A_BANK):
+                row = (h * CHUNKS_A_BANK + i) * SAMPLES
+                nc.tensor.matmul(
+                    out=bank[:, i * P : (i + 1) * P],
+                    lhsT=identity_bf[:, row : row + 1].to_broadcast([P, P]),
+                    rhs=class_bias[:],
+                    start=True,
+                    stop=True,
+                )
+            nc.vector.tensor_copy(out=bias_sb[:, h * BANK : (h + 1) * BANK], in_=bank[:])
+            bias_bank.append(bank)
+
+        result = [keep.tile([P, D], F32, name="result%d" % p) for p in range(PATCHES)]
+        for p in range(PATCHES):
+            if p % VECTOR_EVERY != 0:
+                nc.gpsimd.tensor_tensor(out=result[p][:], in0=residual[p][:], in1=bias_sb[:], op=ADD)
+
+        def add_bias_on_vector(p):
+            for h in range(HALVES):
+                cols = slice(h * BANK, (h + 1) * BANK)
+                nc.vector.tensor_tensor(
+                    out=result[p][:, cols], in0=bias_bank[h][:], in1=residual[p][:, cols], op=ADD
+                )
+
+        grouped = {}
+        codes = {}
+        code_scales = {}
+
+        def regroup(j):
+            words = tokens[j].bitcast(F32)
+            turned = turned_banks.tile([P, PASSES, PAIRS, P], F32, name="turned")
+            for g in range(PASSES):
+                for u in range(PAIRS):
+                    nc.tensor.transpose(
+                        turned[:, g, u, :],
+                        words[:, g * PAIRS * P + u : (g + 1) * PAIRS * P : PAIRS],
+                        identity[:],
+                    )
+            grouped[j] = ring.tile([P, D], BF16, name="grouped", align_bytes=64)
+            nc.scalar.copy(
+                out=grouped[j][:].bitcast(F32).rearrange("p (g r u) -> p g r u", g=PASSES, u=PAIRS),
+                in_=turned[:].rearrange("p g u r -> p g r u"),
+            )
+
+        def quantise(j):
+            codes[j] = ring.tile([P, PASSES * P], U32, name="codes", align_bytes=64)
+            code_scales[j] = ring.tile([P, PASSES * P], U8, name="code_scales", align_bytes=64)
+            nc.vector.quantize_mx(
+                out=codes[j][:].bitcast(FP8X4), scales=code_scales[j][:], in_=grouped[j][:]
+            )
+
+        def multiply_patch(p):
+            j = 1 + p
+            for h in range(HALVES):
+                cols = slice(h * BANK, (h + 1) * BANK)
+                product = product_banks.tile([P, BANK], F32, name="product")
+                for g in range(PASSES):
+                    toks = slice(g * P, (g + 1) * P)
+                    nc.tensor.matmul_mx(
+                        out=product[:],
+                        lhsT=codes[j][:, toks].bitcast(FP8X4),
+                        lhsT_scale=code_scales[j][:, toks],
+                        rhs=w_words[:, g, 2 * h * BANK : 2 * (h + 1) * BANK].bitcast(FP4X4),
+                        rhs_scale=w_scales[:, g, cols],
+                        start=(g == 0),
+                        stop=(g == PASSES - 1),
+                    )
+                nc.vector.tensor_tensor(
+                    out=result[p][:, cols], in0=product[:], in1=result[p][:, cols], op=ADD
+                )
+            nc.sync.dma_start(out=rows_of_patch(out, p), in_=result[p][:])
+
+        class_sums = keep.tile([P, P], F32, name="class_sums")
+        class_result = keep.tile([P, P], F32, name="class_result")
+
+        def multiply_class_tokens():
+            for bank in range(CHUNKS // CHUNKS_A_BANK):
+                product = product_banks.tile([P, BANK], F32, name="product")
+                for i in range(CHUNKS_A_BANK):
+                    c = bank * CHUNKS_A_BANK + i
+                    for g in range(PASSES):
+                        toks = slice(g * P, (g + 1) * P)
+                        nc.tensor.matmul_mx(
+                            out=product[:, i * P : (i + 1) * P],
+                            lhsT=w_words[:, g, 2 * c * P : 2 * (c + 1) * P].bitcast(FP4X4),
+                            lhsT_scale=w_scales[:, g, c * P : (c + 1) * P],
+                            rhs=codes[0][:, toks].bitcast(FP8X4),
+                            rhs_scale=code_scales[0][:, toks],
+                            start=(g == 0),
+                            stop=(g == PASSES - 1),
+                        )
+                width = CHUNKS_A_BANK * SAMPLES
+                nc.vector.tensor_reduce(
+                    out=class_sums[:, bank * width : (bank + 1) * width],
+                    in_=product[:].rearrange("p (m t) -> p m t", t=FRAMES),
+                    axis=mybir.AxisListType.X,
+                    op=ADD,
+                )
+
+        def finish_class_tokens():
+            nc.vector.tensor_tensor(out=class_result[:], in0=class_residual[:], in1=class_bias[:], op=ADD)
+            rows = product_banks.tile([P, BANK], F32, name="product")
+            nc.tensor.transpose(rows[:, 0:P], class_sums[:], identity[:])
+            nc.vector.scalar_tensor_tensor(
+                out=class_result[:],
+                in0=rows[:, 0:P],
+                scalar=1.0 / FRAMES,
+                in1=class_result[:],
+                op0=MULT,
+                op1=ADD,
+            )
+            nc.sync.dma_start(
+                out=out[:, 0, :].rearrange("b (c n) -> c b n", c=CHUNKS), in_=class_result[:]
+            )
+
+        regroup(0)
+        quantise(0)
+        for j in range(1, 1 + ROUND):
+            regroup(j)
+        for j in range(1, 1 + ROUND):
+            quantise(j)
+        add_bias_on_vector(0)
+        multiply_class_tokens()
+        for first in range(1, TILES, ROUND):
+            following = range(first + ROUND, min(first + 2 * ROUND, TILES))
+            for j in following:
+                regroup(j)
+            if first == 1:
+                finish_class_tokens()
+            multiply_patch(first - 1)
+            for j in following:
+                quantise(j)
+            multiply_patch(first)
+            for j in following:
+                if (j - 1) % VECTOR_EVERY == 0:
+                    add_bias_on_vector(j - 1)

@@ -27,7 +27,7 @@ HALVES = D // BANK
 CHUNKS = D // P
 CHUNKS_A_BANK = BANK // P
 ROUND = 2
-VECTOR_EVERY = 3
+VECTOR_EVERY = 2
 
 FLOPS = 2 * TILES * P * D * D
 

@@ -27,7 +27,7 @@ HALVES = D // BANK
 CHUNKS = D // P
 CHUNKS_A_BANK = BANK // P
 ROUND = 2
-VECTOR_EVERY = 2
+VECTOR_EVERY = 3
 
 FLOPS = 2 * TILES * P * D * D
 
@@ -46,15 +46,20 @@ def tile_timesformerlayer_pc_kernel(
 
         w_scales = keep.tile([P, PASSES, D], U8, name="w_scales", align_bytes=64)
         nc.vector.memset(w_scales[:].rearrange("p g n -> p (g n)").bitcast(I32), 0)
+        bias_chunks = keep.tile([P, P], BF16, name="bias_chunks")
+        nc.vector.memset(bias_chunks[:], 0.0)
         identity_bf = keep.tile([P, P], BF16, name="identity_bf")
         make_identity(nc, identity_bf[:])
         identity = keep.tile([P, P], F32, name="identity")
         make_identity(nc, identity[:])
+        chunk_of_row = keep.tile([P, P], BF16, name="chunk_of_row")
+        nc.vector.tensor_copy(
+            out=chunk_of_row[:].rearrange("p (c b) -> p c b", b=SAMPLES),
+            in_=identity_bf[:, 0:CHUNKS].unsqueeze(2).to_broadcast([P, CHUNKS, SAMPLES]),
+        )
 
-        class_bias = keep.tile([P, P], BF16, name="class_bias")
         nc.scalar.dma_start(
-            out=class_bias[:],
-            in_=s_out_b.rearrange("(c n) -> c n", c=CHUNKS).unsqueeze(1).to_broadcast([CHUNKS, SAMPLES, P]),
+            out=bias_chunks[0:CHUNKS, :], in_=s_out_b.rearrange("(c n) -> c n", c=CHUNKS)
         )
         class_residual = keep.tile([P, P], BF16, name="class_residual")
         nc.scalar.dma_start(
@@ -97,24 +102,34 @@ def tile_timesformerlayer_pc_kernel(
                 residual.append(rows)
         bias_bank = []
         bias_sb = keep.tile([P, D], F32, name="bias_sb")
-        for h in range(HALVES):
-            bank = bias_banks.tile([P, BANK], F32, name="bias_bank%d" % h)
-            for i in range(CHUNKS_A_BANK):
-                row = (h * CHUNKS_A_BANK + i) * SAMPLES
-                nc.tensor.matmul(
-                    out=bank[:, i * P : (i + 1) * P],
-                    lhsT=identity_bf[:, row : row + 1].to_broadcast([P, P]),
-                    rhs=class_bias[:],
-                    start=True,
-                    stop=True,
-                )
-            nc.vector.tensor_copy(out=bias_sb[:, h * BANK : (h + 1) * BANK], in_=bank[:])
-            bias_bank.append(bank)
-
         result = [keep.tile([P, D], F32, name="result%d" % p) for p in range(PATCHES)]
-        for p in range(PATCHES):
-            if p % VECTOR_EVERY != 0:
-                nc.gpsimd.tensor_tensor(out=result[p][:], in0=residual[p][:], in1=bias_sb[:], op=ADD)
+
+        def spread_bias():
+            for h in range(HALVES):
+                bank = bias_banks.tile([P, BANK], F32, name="bias_bank%d" % h)
+                for i in range(CHUNKS_A_BANK):
+                    c = h * CHUNKS_A_BANK + i
+                    nc.tensor.matmul(
+                        out=bank[:, i * P : (i + 1) * P],
+                        lhsT=identity_bf[:, c : c + 1].to_broadcast([P, P]),
+                        rhs=bias_chunks[:],
+                        start=True,
+                        stop=True,
+                    )
+                nc.vector.tensor_copy(out=bias_sb[:, h * BANK : (h + 1) * BANK], in_=bank[:])
+                bias_bank.append(bank)
+            class_bias = product_banks.tile([P, BANK], F32, name="product")
+            nc.tensor.matmul(
+                out=class_bias[:, 0:P], lhsT=chunk_of_row[:], rhs=bias_chunks[:], start=True, stop=True
+            )
+            nc.vector.tensor_tensor(
+                out=class_result[:], in0=class_bias[:, 0:P], in1=class_residual[:], op=ADD
+            )
+
+        def add_bias_on_gpsimd():
+            for p in range(PATCHES):
+                if p % VECTOR_EVERY != 0:
+                    nc.gpsimd.tensor_tensor(out=result[p][:], in0=residual[p][:], in1=bias_sb[:], op=ADD)
 
         def add_bias_on_vector(p):
             for h in range(HALVES):
@@ -199,7 +214,6 @@ def tile_timesformerlayer_pc_kernel(
                 )
 
         def finish_class_tokens():
-            nc.vector.tensor_tensor(out=class_result[:], in0=class_residual[:], in1=class_bias[:], op=ADD)
             rows = product_banks.tile([P, BANK], F32, name="product")
             nc.tensor.transpose(rows[:, 0:P], class_sums[:], identity[:])
             nc.vector.scalar_tensor_tensor(
@@ -218,6 +232,8 @@ def tile_timesformerlayer_pc_kernel(
         quantise(0)
         for j in range(1, 1 + ROUND):
             regroup(j)
+        spread_bias()
+        add_bias_on_gpsimd()
         for j in range(1, 1 + ROUND):
             quantise(j)
         add_bias_on_vector(0)

@@ -26,7 +26,9 @@ BANK = 512
 HALVES = D // BANK
 CHUNKS = D // P
 CHUNKS_A_BANK = BANK // P
-ROUND = 2
+ROUND = 4
+TURNED_BANKS = 2
+PRODUCT_BANKS = 4
 VECTOR_EVERY = 3
 
 FLOPS = 2 * TILES * P * D * D
@@ -39,8 +41,8 @@ def tile_timesformerlayer_pc_kernel(
     with ExitStack() as stack:
         keep = stack.enter_context(tc.tile_pool(name="keep", bufs=1))
         ring = stack.enter_context(tc.tile_pool(name="ring", bufs=2 * ROUND))
-        turned_banks = stack.enter_context(tc.psum_pool(name="turned_banks", bufs=ROUND))
-        product_banks = stack.enter_context(tc.psum_pool(name="product_banks", bufs=ROUND * HALVES))
+        turned_banks = stack.enter_context(tc.psum_pool(name="turned_banks", bufs=TURNED_BANKS))
+        product_banks = stack.enter_context(tc.psum_pool(name="product_banks", bufs=PRODUCT_BANKS))
         bias_banks = stack.enter_context(tc.psum_pool(name="bias_banks", bufs=1))
         stack.enter_context(tc.manual_schedule())
 
@@ -131,12 +133,15 @@ def tile_timesformerlayer_pc_kernel(
                 if p % VECTOR_EVERY != 0:
                     nc.gpsimd.tensor_tensor(out=result[p][:], in0=residual[p][:], in1=bias_sb[:], op=ADD)
 
-        def add_bias_on_vector(p):
-            for h in range(HALVES):
-                cols = slice(h * BANK, (h + 1) * BANK)
-                nc.vector.tensor_tensor(
-                    out=result[p][:, cols], in0=bias_bank[h][:], in1=residual[p][:, cols], op=ADD
-                )
+        def add_bias_on_vector(tiles):
+            for j in tiles:
+                p = j - 1
+                if p % VECTOR_EVERY == 0:
+                    for h in range(HALVES):
+                        cols = slice(h * BANK, (h + 1) * BANK)
+                        nc.vector.tensor_tensor(
+                            out=result[p][:, cols], in0=bias_bank[h][:], in1=residual[p][:, cols], op=ADD
+                        )
 
         grouped = {}
         codes = {}
@@ -236,18 +241,17 @@ def tile_timesformerlayer_pc_kernel(
         add_bias_on_gpsimd()
         for j in range(1, 1 + ROUND):
             quantise(j)
-        add_bias_on_vector(0)
         multiply_class_tokens()
+        add_bias_on_vector(range(1, 1 + ROUND))
         for first in range(1, TILES, ROUND):
             following = range(first + ROUND, min(first + 2 * ROUND, TILES))
             for j in following:
                 regroup(j)
             if first == 1:
                 finish_class_tokens()
-            multiply_patch(first - 1)
-            for j in following:
-                quantise(j)
-            multiply_patch(first)
-            for j in following:
-                if (j - 1) % VECTOR_EVERY == 0:
-                    add_bias_on_vector(j - 1)
+            for j in range(first, first + ROUND):
+                multiply_patch(j - 1)
+                if j == first + ROUND // 2 - 1:
+                    for nxt in following:
+                        quantise(nxt)
+            add_bias_on_vector(following)

@@ -26,9 +26,10 @@ BANK = 512
 HALVES = D // BANK
 CHUNKS = D // P
 CHUNKS_A_BANK = BANK // P
-ROUND = 4
+GROUP = 2
+GROUPS = PATCHES // GROUP
 TURNED_BANKS = 2
-PRODUCT_BANKS = 4
+PRODUCT_BANKS = 6
 VECTOR_EVERY = 3
 
 FLOPS = 2 * TILES * P * D * D
@@ -40,9 +41,7 @@ def tile_timesformerlayer_pc_kernel(
     nc = tc.nc
     with ExitStack() as stack:
         keep = stack.enter_context(tc.tile_pool(name="keep", bufs=1))
-        ring = stack.enter_context(tc.tile_pool(name="ring", bufs=2 * ROUND))
-        turned_banks = stack.enter_context(tc.psum_pool(name="turned_banks", bufs=TURNED_BANKS))
-        product_banks = stack.enter_context(tc.psum_pool(name="product_banks", bufs=PRODUCT_BANKS))
+        ring = stack.enter_context(tc.tile_pool(name="ring", bufs=4))
         bias_banks = stack.enter_context(tc.psum_pool(name="bias_banks", bufs=1))
         stack.enter_context(tc.manual_schedule())
 
@@ -50,10 +49,10 @@ def tile_timesformerlayer_pc_kernel(
         nc.vector.memset(w_scales[:].rearrange("p g n -> p (g n)").bitcast(I32), 0)
         bias_chunks = keep.tile([P, P], BF16, name="bias_chunks")
         nc.vector.memset(bias_chunks[:], 0.0)
-        identity_bf = keep.tile([P, P], BF16, name="identity_bf")
-        make_identity(nc, identity_bf[:])
         identity = keep.tile([P, P], F32, name="identity")
         make_identity(nc, identity[:])
+        identity_bf = keep.tile([P, P], BF16, name="identity_bf")
+        make_identity(nc, identity_bf[:])
         chunk_of_row = keep.tile([P, P], BF16, name="chunk_of_row")
         nc.vector.tensor_copy(
             out=chunk_of_row[:].rearrange("p (c b) -> p c b", b=SAMPLES),
@@ -68,21 +67,27 @@ def tile_timesformerlayer_pc_kernel(
             out=class_residual[:], in_=x_res[:, 0, :].rearrange("b (c n) -> c b n", c=CHUNKS)
         )
 
-        tokens = []
-        class_tokens = keep.tile([P, D], BF16, name="class_tokens")
-        nc.sync.dma_start(out=class_tokens[:], in_=ctx_s[:, 0, :])
-        tokens.append(class_tokens[:])
-
-        def load_tokens(first):
-            both = keep.tile([P, ROUND, D], BF16, name="tokens%d" % first)
-            nc.sync.dma_start(out=both[:], in_=ctx_s[:, first : first + ROUND, :])
-            for i in range(ROUND):
-                tokens.append(both[:, i, :])
-
         def rows_of_patch(tensor, p):
             return tensor[:, 1 + p * FRAMES : 1 + (p + 1) * FRAMES, :]
 
-        load_tokens(1)
+        tokens = []
+        residual = []
+
+        def load_residual(p):
+            rows = keep.tile([P, D], BF16, name="residual%d" % p)
+            nc.sync.dma_start(out=rows[:], in_=rows_of_patch(x_res, p))
+            residual.append(rows)
+
+        class_tokens = keep.tile([P, D], BF16, name="class_tokens")
+        nc.sync.dma_start(out=class_tokens[:], in_=ctx_s[:, 0, :])
+        tokens.append(class_tokens[:])
+        for r in range(GROUPS):
+            group = keep.tile([P, GROUP, D], BF16, name="tokens%d" % r)
+            nc.sync.dma_start(out=group[:], in_=ctx_s[:, 1 + r * GROUP : 1 + (r + 1) * GROUP, :])
+            for i in range(GROUP):
+                tokens.append(group[:, i, :])
+            if r > 0:
+                load_residual(r - 1)
         w_words = keep.tile([P, PASSES, 2 * D], U8, name="w_words", align_bytes=64)
         nc.sync.dma_start(
             out=w_words[:].bitcast(I32), in_=s_out_w_words.rearrange("g p n -> p g n").bitcast(I32)
@@ -94,17 +99,14 @@ def tile_timesformerlayer_pc_kernel(
                 .rearrange("g r n -> r g n")
                 .bitcast(I32),
             )
-        residual = []
-        for first in range(1, TILES, ROUND):
-            if first + ROUND < TILES:
-                load_tokens(first + ROUND)
-            for p in range(first - 1, first - 1 + ROUND):
-                rows = keep.tile([P, D], BF16, name="residual%d" % p)
-                nc.sync.dma_start(out=rows[:], in_=rows_of_patch(x_res, p))
-                residual.append(rows)
+        for p in range(GROUPS - 1, PATCHES):
+            load_residual(p)
+
         bias_bank = []
         bias_sb = keep.tile([P, D], F32, name="bias_sb")
         result = [keep.tile([P, D], F32, name="result%d" % p) for p in range(PATCHES)]
+        codes = []
+        code_scales = []
 
         def spread_bias():
             for h in range(HALVES):
@@ -120,6 +122,56 @@ def tile_timesformerlayer_pc_kernel(
                     )
                 nc.vector.tensor_copy(out=bias_sb[:, h * BANK : (h + 1) * BANK], in_=bank[:])
                 bias_bank.append(bank)
+
+        def add_bias_on_gpsimd():
+            for p in range(PATCHES):
+                if p % VECTOR_EVERY != 0:
+                    nc.gpsimd.tensor_tensor(out=result[p][:], in0=residual[p][:], in1=bias_sb[:], op=ADD)
+
+        def add_bias_on_vector(p):
+            if p % VECTOR_EVERY == 0:
+                for h in range(HALVES):
+                    cols = slice(h * BANK, (h + 1) * BANK)
+                    nc.vector.tensor_tensor(
+                        out=result[p][:, cols], in0=bias_bank[h][:], in1=residual[p][:, cols], op=ADD
+                    )
+
+        with tc.psum_pool(name="turned_banks", bufs=TURNED_BANKS) as turned_banks:
+
+            def prepare(j):
+                words = tokens[j].bitcast(F32)
+                turned = turned_banks.tile([P, PASSES, PAIRS, P], F32, name="turned")
+                for g in range(PASSES):
+                    for u in range(PAIRS):
+                        nc.tensor.transpose(
+                            turned[:, g, u, :],
+                            words[:, g * PAIRS * P + u : (g + 1) * PAIRS * P : PAIRS],
+                            identity[:],
+                        )
+                grouped = ring.tile([P, D], BF16, name="grouped", align_bytes=64)
+                nc.scalar.copy(
+                    out=grouped[:].bitcast(F32).rearrange("p (g r u) -> p g r u", g=PASSES, u=PAIRS),
+                    in_=turned[:].rearrange("p g u r -> p g r u"),
+                )
+                codes.append(keep.tile([P, PASSES * P], U32, name="codes%d" % j, align_bytes=64))
+                code_scales.append(keep.tile([P, PASSES * P], U8, name="code_scales%d" % j, align_bytes=64))
+                nc.vector.quantize_mx(
+                    out=codes[j][:].bitcast(FP8X4), scales=code_scales[j][:], in_=grouped[:]
+                )
+
+            prepare(0)
+            spread_bias()
+            add_bias_on_gpsimd()
+            for r in range(GROUPS):
+                for j in range(1 + r * GROUP, 1 + (r + 1) * GROUP):
+                    prepare(j)
+                if r > 0:
+                    add_bias_on_vector(r - 1)
+            for p in range(GROUPS - 1, PATCHES):
+                add_bias_on_vector(p)
+
+        with tc.psum_pool(name="product_banks", bufs=PRODUCT_BANKS, reuse_waits="tile") as product_banks:
+            class_result = keep.tile([P, P], F32, name="class_result")
             class_bias = product_banks.tile([P, BANK], F32, name="product")
             nc.tensor.matmul(
                 out=class_bias[:, 0:P], lhsT=chunk_of_row[:], rhs=bias_chunks[:], start=True, stop=True
@@ -127,74 +179,7 @@ def tile_timesformerlayer_pc_kernel(
             nc.vector.tensor_tensor(
                 out=class_result[:], in0=class_bias[:, 0:P], in1=class_residual[:], op=ADD
             )
-
-        def add_bias_on_gpsimd():
-            for p in range(PATCHES):
-                if p % VECTOR_EVERY != 0:
-                    nc.gpsimd.tensor_tensor(out=result[p][:], in0=residual[p][:], in1=bias_sb[:], op=ADD)
-
-        def add_bias_on_vector(tiles):
-            for j in tiles:
-                p = j - 1
-                if p % VECTOR_EVERY == 0:
-                    for h in range(HALVES):
-                        cols = slice(h * BANK, (h + 1) * BANK)
-                        nc.vector.tensor_tensor(
-                            out=result[p][:, cols], in0=bias_bank[h][:], in1=residual[p][:, cols], op=ADD
-                        )
-
-        grouped = {}
-        codes = {}
-        code_scales = {}
-
-        def regroup(j):
-            words = tokens[j].bitcast(F32)
-            turned = turned_banks.tile([P, PASSES, PAIRS, P], F32, name="turned")
-            for g in range(PASSES):
-                for u in range(PAIRS):
-                    nc.tensor.transpose(
-                        turned[:, g, u, :],
-                        words[:, g * PAIRS * P + u : (g + 1) * PAIRS * P : PAIRS],
-                        identity[:],
-                    )
-            grouped[j] = ring.tile([P, D], BF16, name="grouped", align_bytes=64)
-            nc.scalar.copy(
-                out=grouped[j][:].bitcast(F32).rearrange("p (g r u) -> p g r u", g=PASSES, u=PAIRS),
-                in_=turned[:].rearrange("p g u r -> p g r u"),
-            )
-
-        def quantise(j):
-            codes[j] = ring.tile([P, PASSES * P], U32, name="codes", align_bytes=64)
-            code_scales[j] = ring.tile([P, PASSES * P], U8, name="code_scales", align_bytes=64)
-            nc.vector.quantize_mx(
-                out=codes[j][:].bitcast(FP8X4), scales=code_scales[j][:], in_=grouped[j][:]
-            )
-
-        def multiply_patch(p):
-            j = 1 + p
-            for h in range(HALVES):
-                cols = slice(h * BANK, (h + 1) * BANK)
-                product = product_banks.tile([P, BANK], F32, name="product")
-                for g in range(PASSES):
-                    toks = slice(g * P, (g + 1) * P)
-                    nc.tensor.matmul_mx(
-                        out=product[:],
-                        lhsT=codes[j][:, toks].bitcast(FP8X4),
-                        lhsT_scale=code_scales[j][:, toks],
-                        rhs=w_words[:, g, 2 * h * BANK : 2 * (h + 1) * BANK].bitcast(FP4X4),
-                        rhs_scale=w_scales[:, g, cols],
-                        start=(g == 0),
-                        stop=(g == PASSES - 1),
-                    )
-                nc.vector.tensor_tensor(
-                    out=result[p][:, cols], in0=product[:], in1=result[p][:, cols], op=ADD
-                )
-            nc.sync.dma_start(out=rows_of_patch(out, p), in_=result[p][:])
-
-        class_sums = keep.tile([P, P], F32, name="class_sums")
-        class_result = keep.tile([P, P], F32, name="class_result")
-
-        def multiply_class_tokens():
+            class_sums = keep.tile([P, P], F32, name="class_sums")
             for bank in range(CHUNKS // CHUNKS_A_BANK):
                 product = product_banks.tile([P, BANK], F32, name="product")
                 for i in range(CHUNKS_A_BANK):
@@ -218,7 +203,27 @@ def tile_timesformerlayer_pc_kernel(
                     op=ADD,
                 )
 
-        def finish_class_tokens():
+            for p in range(PATCHES):
+                j = 1 + p
+                for h in range(HALVES):
+                    cols = slice(h * BANK, (h + 1) * BANK)
+                    product = product_banks.tile([P, BANK], F32, name="product")
+                    for g in range(PASSES):
+                        toks = slice(g * P, (g + 1) * P)
+                        nc.tensor.matmul_mx(
+                            out=product[:],
+                            lhsT=codes[j][:, toks].bitcast(FP8X4),
+                            lhsT_scale=code_scales[j][:, toks],
+                            rhs=w_words[:, g, 2 * h * BANK : 2 * (h + 1) * BANK].bitcast(FP4X4),
+                            rhs_scale=w_scales[:, g, cols],
+                            start=(g == 0),
+                            stop=(g == PASSES - 1),
+                        )
+                    nc.vector.tensor_tensor(
+                        out=result[p][:, cols], in0=product[:], in1=result[p][:, cols], op=ADD
+                    )
+                nc.sync.dma_start(out=rows_of_patch(out, p), in_=result[p][:])
+
             rows = product_banks.tile([P, BANK], F32, name="product")
             nc.tensor.transpose(rows[:, 0:P], class_sums[:], identity[:])
             nc.vector.scalar_tensor_tensor(
@@ -232,26 +237,3 @@ def tile_timesformerlayer_pc_kernel(
             nc.sync.dma_start(
                 out=out[:, 0, :].rearrange("b (c n) -> c b n", c=CHUNKS), in_=class_result[:]
             )
-
-        regroup(0)
-        quantise(0)
-        for j in range(1, 1 + ROUND):
-            regroup(j)
-        spread_bias()
-        add_bias_on_gpsimd()
-        for j in range(1, 1 + ROUND):
-            quantise(j)
-        multiply_class_tokens()
-        add_bias_on_vector(range(1, 1 + ROUND))
-        for first in range(1, TILES, ROUND):
-            following = range(first + ROUND, min(first + 2 * ROUND, TILES))
-            for j in following:
-                regroup(j)
-            if first == 1:
-                finish_class_tokens()
-            for j in range(first, first + ROUND):
-                multiply_patch(j - 1)
-                if j == first + ROUND // 2 - 1:
-                    for nxt in following:
-                        quantise(nxt)
-            add_bias_on_vector(following)

@@ -28,9 +28,9 @@ CHUNKS = D // P
 CHUNKS_A_BANK = BANK // P
 GROUP = 2
 GROUPS = PATCHES // GROUP
-TURNED_BANKS = 2
+TURNED_BANKS = 4
 PRODUCT_BANKS = 6
-VECTOR_EVERY = 3
+VECTOR_PATCHES = GROUPS
 
 FLOPS = 2 * TILES * P * D * D
 
@@ -86,8 +86,7 @@ def tile_timesformerlayer_pc_kernel(
             nc.sync.dma_start(out=group[:], in_=ctx_s[:, 1 + r * GROUP : 1 + (r + 1) * GROUP, :])
             for i in range(GROUP):
                 tokens.append(group[:, i, :])
-            if r > 0:
-                load_residual(r - 1)
+            load_residual(r)
         w_words = keep.tile([P, PASSES, 2 * D], U8, name="w_words", align_bytes=64)
         nc.sync.dma_start(
             out=w_words[:].bitcast(I32), in_=s_out_w_words.rearrange("g p n -> p g n").bitcast(I32)
@@ -99,7 +98,7 @@ def tile_timesformerlayer_pc_kernel(
                 .rearrange("g r n -> r g n")
                 .bitcast(I32),
             )
-        for p in range(GROUPS - 1, PATCHES):
+        for p in range(VECTOR_PATCHES, PATCHES):
             load_residual(p)
 
         bias_bank = []
@@ -120,21 +119,20 @@ def tile_timesformerlayer_pc_kernel(
                         start=True,
                         stop=True,
                     )
-                nc.vector.tensor_copy(out=bias_sb[:, h * BANK : (h + 1) * BANK], in_=bank[:])
                 bias_bank.append(bank)
 
-        def add_bias_on_gpsimd():
-            for p in range(PATCHES):
-                if p % VECTOR_EVERY != 0:
-                    nc.gpsimd.tensor_tensor(out=result[p][:], in0=residual[p][:], in1=bias_sb[:], op=ADD)
-
         def add_bias_on_vector(p):
-            if p % VECTOR_EVERY == 0:
-                for h in range(HALVES):
-                    cols = slice(h * BANK, (h + 1) * BANK)
-                    nc.vector.tensor_tensor(
-                        out=result[p][:, cols], in0=bias_bank[h][:], in1=residual[p][:, cols], op=ADD
-                    )
+            for h in range(HALVES):
+                cols = slice(h * BANK, (h + 1) * BANK)
+                nc.vector.tensor_tensor(
+                    out=result[p][:, cols], in0=bias_bank[h][:], in1=residual[p][:, cols], op=ADD
+                )
+
+        def add_bias_on_gpsimd():
+            for h in range(HALVES):
+                nc.vector.tensor_copy(out=bias_sb[:, h * BANK : (h + 1) * BANK], in_=bias_bank[h][:])
+            for p in range(VECTOR_PATCHES, PATCHES):
+                nc.gpsimd.tensor_tensor(out=result[p][:], in0=residual[p][:], in1=bias_sb[:], op=ADD)
 
         with tc.psum_pool(name="turned_banks", bufs=TURNED_BANKS) as turned_banks:
 
@@ -159,16 +157,18 @@ def tile_timesformerlayer_pc_kernel(
                     out=codes[j][:].bitcast(FP8X4), scales=code_scales[j][:], in_=grouped[:]
                 )
 
-            prepare(0)
-            spread_bias()
-            add_bias_on_gpsimd()
-            for r in range(GROUPS):
+            def prepare_group(r):
                 for j in range(1 + r * GROUP, 1 + (r + 1) * GROUP):
                     prepare(j)
-                if r > 0:
-                    add_bias_on_vector(r - 1)
-            for p in range(GROUPS - 1, PATCHES):
-                add_bias_on_vector(p)
+
+            prepare(0)
+            prepare_group(0)
+            spread_bias()
+            for r in range(1, GROUPS):
+                add_bias_on_vector(r - 1)
+                prepare_group(r)
+            add_bias_on_gpsimd()
+            add_bias_on_vector(GROUPS - 1)
 
         with tc.psum_pool(name="product_banks", bufs=PRODUCT_BANKS, reuse_waits="tile") as product_banks:
             class_result = keep.tile([P, P], F32, name="class_result")
@@ -222,7 +222,7 @@ def tile_timesformerlayer_pc_kernel(
                     nc.vector.tensor_tensor(
                         out=result[p][:, cols], in0=product[:], in1=result[p][:, cols], op=ADD
                     )
-                nc.sync.dma_start(out=rows_of_patch(out, p), in_=result[p][:])
+                    nc.sync.dma_start(out=rows_of_patch(out, p)[:, :, cols], in_=result[p][:, cols])
 
             rows = product_banks.tile([P, BANK], F32, name="product")
             nc.tensor.transpose(rows[:, 0:P], class_sums[:], identity[:])

@@ -1,7 +1,6 @@
 from contextlib import ExitStack
 
 import concourse.mybir as mybir
-from concourse.masks import make_identity
 
 F32 = mybir.dt.float32
 BF16 = mybir.dt.bfloat16
@@ -12,6 +11,7 @@ FP8X4 = mybir.dt.float8_e4m3fn_x4
 FP4X4 = mybir.dt.float4_e2m1fn_x4
 ADD = mybir.AluOpType.add
 MULT = mybir.AluOpType.mult
+IS_EQUAL = mybir.AluOpType.is_equal
 
 P = 128
 SAMPLES = 16
@@ -26,13 +26,35 @@ BANK = 512
 HALVES = D // BANK
 CHUNKS = D // P
 CHUNKS_A_BANK = BANK // P
-GROUP = 2
-GROUPS = PATCHES // GROUP
-TURNED_BANKS = 4
-PRODUCT_BANKS = 6
-VECTOR_PATCHES = GROUPS
+ROUND = 2
+TURNED_BANKS = 2
+PRODUCT_BANKS = 4
+VECTOR_EVERY = 3
 
 FLOPS = 2 * TILES * P * D * D
+
+
+def identity_by_vector(nc, pool):
+    block = 32
+    ones = pool.tile([P, P], F32, name="ones")
+    nc.vector.memset(ones[:], 1.0)
+    column = pool.tile([P, P], F32, name="column", align_bytes=64)
+    nc.vector.tensor_tensor_scan(
+        out=column[:], data0=ones[:], data1=ones[:], initial=-1.0, op0=MULT, op1=ADD
+    )
+    turned = pool.tile([P, P], F32, name="column_turned", align_bytes=64)
+    nc.vector.transpose(out=turned[:], in_=column[:])
+    identity = pool.tile([P, P], F32, name="identity")
+    for first in range(0, P, block):
+        rows = slice(first, first + block)
+        nc.vector.tensor_scalar(
+            out=identity[rows, :],
+            in0=column[rows, :],
+            scalar1=turned[rows, first : first + 1],
+            scalar2=None,
+            op0=IS_EQUAL,
+        )
+    return identity
 
 
 def tile_timesformerlayer_pc_kernel(
@@ -41,7 +63,9 @@ def tile_timesformerlayer_pc_kernel(
     nc = tc.nc
     with ExitStack() as stack:
         keep = stack.enter_context(tc.tile_pool(name="keep", bufs=1))
-        ring = stack.enter_context(tc.tile_pool(name="ring", bufs=4))
+        ring = stack.enter_context(tc.tile_pool(name="ring", bufs=2 * ROUND))
+        turned_banks = stack.enter_context(tc.psum_pool(name="turned_banks", bufs=TURNED_BANKS))
+        product_banks = stack.enter_context(tc.psum_pool(name="product_banks", bufs=PRODUCT_BANKS))
         bias_banks = stack.enter_context(tc.psum_pool(name="bias_banks", bufs=1))
         stack.enter_context(tc.manual_schedule())
 
@@ -49,10 +73,9 @@ def tile_timesformerlayer_pc_kernel(
         nc.vector.memset(w_scales[:].rearrange("p g n -> p (g n)").bitcast(I32), 0)
         bias_chunks = keep.tile([P, P], BF16, name="bias_chunks")
         nc.vector.memset(bias_chunks[:], 0.0)
-        identity = keep.tile([P, P], F32, name="identity")
-        make_identity(nc, identity[:])
+        identity = identity_by_vector(nc, keep)
         identity_bf = keep.tile([P, P], BF16, name="identity_bf")
-        make_identity(nc, identity_bf[:])
+        nc.vector.tensor_copy(out=identity_bf[:], in_=identity[:])
         chunk_of_row = keep.tile([P, P], BF16, name="chunk_of_row")
         nc.vector.tensor_copy(
             out=chunk_of_row[:].rearrange("p (c b) -> p c b", b=SAMPLES),
@@ -67,26 +90,21 @@ def tile_timesformerlayer_pc_kernel(
             out=class_residual[:], in_=x_res[:, 0, :].rearrange("b (c n) -> c b n", c=CHUNKS)
         )
 
-        def rows_of_patch(tensor, p):
-            return tensor[:, 1 + p * FRAMES : 1 + (p + 1) * FRAMES, :]
-
         tokens = []
-        residual = []
-
-        def load_residual(p):
-            rows = keep.tile([P, D], BF16, name="residual%d" % p)
-            nc.sync.dma_start(out=rows[:], in_=rows_of_patch(x_res, p))
-            residual.append(rows)
-
         class_tokens = keep.tile([P, D], BF16, name="class_tokens")
         nc.sync.dma_start(out=class_tokens[:], in_=ctx_s[:, 0, :])
         tokens.append(class_tokens[:])
-        for r in range(GROUPS):
-            group = keep.tile([P, GROUP, D], BF16, name="tokens%d" % r)
-            nc.sync.dma_start(out=group[:], in_=ctx_s[:, 1 + r * GROUP : 1 + (r + 1) * GROUP, :])
-            for i in range(GROUP):
-                tokens.append(group[:, i, :])
-            load_residual(r)
+
+        def load_tokens(first):
+            both = keep.tile([P, ROUND, D], BF16, name="tokens%d" % first)
+            nc.sync.dma_start(out=both[:], in_=ctx_s[:, first : first + ROUND, :])
+            for i in range(ROUND):
+                tokens.append(both[:, i, :])
+
+        def rows_of_patch(tensor, p):
+            return tensor[:, 1 + p * FRAMES : 1 + (p + 1) * FRAMES, :]
+
+        load_tokens(1)
         w_words = keep.tile([P, PASSES, 2 * D], U8, name="w_words", align_bytes=64)
         nc.sync.dma_start(
             out=w_words[:].bitcast(I32), in_=s_out_w_words.rearrange("g p n -> p g n").bitcast(I32)
@@ -98,14 +116,17 @@ def tile_timesformerlayer_pc_kernel(
                 .rearrange("g r n -> r g n")
                 .bitcast(I32),
             )
-        for p in range(VECTOR_PATCHES, PATCHES):
-            load_residual(p)
-
+        residual = []
+        for first in range(1, TILES, ROUND):
+            if first + ROUND < TILES:
+                load_tokens(first + ROUND)
+            for p in range(first - 1, first - 1 + ROUND):
+                rows = keep.tile([P, D], BF16, name="residual%d" % p)
+                nc.sync.dma_start(out=rows[:], in_=rows_of_patch(x_res, p))
+                residual.append(rows)
         bias_bank = []
         bias_sb = keep.tile([P, D], F32, name="bias_sb")
         result = [keep.tile([P, D], F32, name="result%d" % p) for p in range(PATCHES)]
-        codes = []
-        code_scales = []
 
         def spread_bias():
             for h in range(HALVES):
@@ -119,59 +140,8 @@ def tile_timesformerlayer_pc_kernel(
                         start=True,
                         stop=True,
                     )
+                nc.vector.tensor_copy(out=bias_sb[:, h * BANK : (h + 1) * BANK], in_=bank[:])
                 bias_bank.append(bank)
-
-        def add_bias_on_vector(p):
-            for h in range(HALVES):
-                cols = slice(h * BANK, (h + 1) * BANK)
-                nc.vector.tensor_tensor(
-                    out=result[p][:, cols], in0=bias_bank[h][:], in1=residual[p][:, cols], op=ADD
-                )
-
-        def add_bias_on_gpsimd():
-            for h in range(HALVES):
-                nc.vector.tensor_copy(out=bias_sb[:, h * BANK : (h + 1) * BANK], in_=bias_bank[h][:])
-            for p in range(VECTOR_PATCHES, PATCHES):
-                nc.gpsimd.tensor_tensor(out=result[p][:], in0=residual[p][:], in1=bias_sb[:], op=ADD)
-
-        with tc.psum_pool(name="turned_banks", bufs=TURNED_BANKS) as turned_banks:
-
-            def prepare(j):
-                words = tokens[j].bitcast(F32)
-                turned = turned_banks.tile([P, PASSES, PAIRS, P], F32, name="turned")
-                for g in range(PASSES):
-                    for u in range(PAIRS):
-                        nc.tensor.transpose(
-                            turned[:, g, u, :],
-                            words[:, g * PAIRS * P + u : (g + 1) * PAIRS * P : PAIRS],
-                            identity[:],
-                        )
-                grouped = ring.tile([P, D], BF16, name="grouped", align_bytes=64)
-                nc.scalar.copy(
-                    out=grouped[:].bitcast(F32).rearrange("p (g r u) -> p g r u", g=PASSES, u=PAIRS),
-                    in_=turned[:].rearrange("p g u r -> p g r u"),
-                )
-                codes.append(keep.tile([P, PASSES * P], U32, name="codes%d" % j, align_bytes=64))
-                code_scales.append(keep.tile([P, PASSES * P], U8, name="code_scales%d" % j, align_bytes=64))
-                nc.vector.quantize_mx(
-                    out=codes[j][:].bitcast(FP8X4), scales=code_scales[j][:], in_=grouped[:]
-                )
-
-            def prepare_group(r):
-                for j in range(1 + r * GROUP, 1 + (r + 1) * GROUP):
-                    prepare(j)
-
-            prepare(0)
-            prepare_group(0)
-            spread_bias()
-            for r in range(1, GROUPS):
-                add_bias_on_vector(r - 1)
-                prepare_group(r)
-            add_bias_on_gpsimd()
-            add_bias_on_vector(GROUPS - 1)
-
-        with tc.psum_pool(name="product_banks", bufs=PRODUCT_BANKS, reuse_waits="tile") as product_banks:
-            class_result = keep.tile([P, P], F32, name="class_result")
             class_bias = product_banks.tile([P, BANK], F32, name="product")
             nc.tensor.matmul(
                 out=class_bias[:, 0:P], lhsT=chunk_of_row[:], rhs=bias_chunks[:], start=True, stop=True
@@ -179,7 +149,74 @@ def tile_timesformerlayer_pc_kernel(
             nc.vector.tensor_tensor(
                 out=class_result[:], in0=class_bias[:, 0:P], in1=class_residual[:], op=ADD
             )
-            class_sums = keep.tile([P, P], F32, name="class_sums")
+
+        def add_bias_on_gpsimd():
+            for p in range(PATCHES):
+                if p % VECTOR_EVERY != 0:
+                    nc.gpsimd.tensor_tensor(out=result[p][:], in0=residual[p][:], in1=bias_sb[:], op=ADD)
+
+        def add_bias_on_vector(tiles):
+            for j in tiles:
+                p = j - 1
+                if p % VECTOR_EVERY == 0:
+                    for h in range(HALVES):
+                        cols = slice(h * BANK, (h + 1) * BANK)
+                        nc.vector.tensor_tensor(
+                            out=result[p][:, cols], in0=bias_bank[h][:], in1=residual[p][:, cols], op=ADD
+                        )
+
+        grouped = {}
+        codes = {}
+        code_scales = {}
+
+        def regroup(j):
+            words = tokens[j].bitcast(F32)
+            turned = turned_banks.tile([P, PASSES, PAIRS, P], F32, name="turned")
+            for g in range(PASSES):
+                for u in range(PAIRS):
+                    nc.tensor.transpose(
+                        turned[:, g, u, :],
+                        words[:, g * PAIRS * P + u : (g + 1) * PAIRS * P : PAIRS],
+                        identity[:],
+                    )
+            grouped[j] = ring.tile([P, D], BF16, name="grouped", align_bytes=64)
+            nc.scalar.copy(
+                out=grouped[j][:].bitcast(F32).rearrange("p (g r u) -> p g r u", g=PASSES, u=PAIRS),
+                in_=turned[:].rearrange("p g u r -> p g r u"),
+            )
+
+        def quantise(j):
+            codes[j] = ring.tile([P, PASSES * P], U32, name="codes", align_bytes=64)
+            code_scales[j] = ring.tile([P, PASSES * P], U8, name="code_scales", align_bytes=64)
+            nc.vector.quantize_mx(
+                out=codes[j][:].bitcast(FP8X4), scales=code_scales[j][:], in_=grouped[j][:]
+            )
+
+        def multiply_patch(p):
+            j = 1 + p
+            for h in range(HALVES):
+                cols = slice(h * BANK, (h + 1) * BANK)
+                product = product_banks.tile([P, BANK], F32, name="product")
+                for g in range(PASSES):
+                    toks = slice(g * P, (g + 1) * P)
+                    nc.tensor.matmul_mx(
+                        out=product[:],
+                        lhsT=codes[j][:, toks].bitcast(FP8X4),
+                        lhsT_scale=code_scales[j][:, toks],
+                        rhs=w_words[:, g, 2 * h * BANK : 2 * (h + 1) * BANK].bitcast(FP4X4),
+                        rhs_scale=w_scales[:, g, cols],
+                        start=(g == 0),
+                        stop=(g == PASSES - 1),
+                    )
+                nc.vector.tensor_tensor(
+                    out=result[p][:, cols], in0=product[:], in1=result[p][:, cols], op=ADD
+                )
+            nc.sync.dma_start(out=rows_of_patch(out, p), in_=result[p][:])
+
+        class_sums = keep.tile([P, P], F32, name="class_sums")
+        class_result = keep.tile([P, P], F32, name="class_result")
+
+        def multiply_class_tokens():
             for bank in range(CHUNKS // CHUNKS_A_BANK):
                 product = product_banks.tile([P, BANK], F32, name="product")
                 for i in range(CHUNKS_A_BANK):
@@ -203,27 +240,7 @@ def tile_timesformerlayer_pc_kernel(
                     op=ADD,
                 )
 
-            for p in range(PATCHES):
-                j = 1 + p
-                for h in range(HALVES):
-                    cols = slice(h * BANK, (h + 1) * BANK)
-                    product = product_banks.tile([P, BANK], F32, name="product")
-                    for g in range(PASSES):
-                        toks = slice(g * P, (g + 1) * P)
-                        nc.tensor.matmul_mx(
-                            out=product[:],
-                            lhsT=codes[j][:, toks].bitcast(FP8X4),
-                            lhsT_scale=code_scales[j][:, toks],
-                            rhs=w_words[:, g, 2 * h * BANK : 2 * (h + 1) * BANK].bitcast(FP4X4),
-                            rhs_scale=w_scales[:, g, cols],
-                            start=(g == 0),
-                            stop=(g == PASSES - 1),
-                        )
-                    nc.vector.tensor_tensor(
-                        out=result[p][:, cols], in0=product[:], in1=result[p][:, cols], op=ADD
-                    )
-                    nc.sync.dma_start(out=rows_of_patch(out, p)[:, :, cols], in_=result[p][:, cols])
-
+        def finish_class_tokens():
             rows = product_banks.tile([P, BANK], F32, name="product")
             nc.tensor.transpose(rows[:, 0:P], class_sums[:], identity[:])
             nc.vector.scalar_tensor_tensor(
@@ -237,3 +254,26 @@ def tile_timesformerlayer_pc_kernel(
             nc.sync.dma_start(
                 out=out[:, 0, :].rearrange("b (c n) -> c b n", c=CHUNKS), in_=class_result[:]
             )
+
+        regroup(0)
+        quantise(0)
+        for j in range(1, 1 + ROUND):
+            regroup(j)
+        spread_bias()
+        add_bias_on_gpsimd()
+        for j in range(1, 1 + ROUND):
+            quantise(j)
+        multiply_class_tokens()
+        add_bias_on_vector(range(1, 1 + ROUND))
+        for first in range(1, TILES, ROUND):
+            following = range(first + ROUND, min(first + 2 * ROUND, TILES))
+            for j in following:
+                regroup(j)
+            if first == 1:
+                finish_class_tokens()
+            for j in range(first, first + ROUND):
+                multiply_patch(j - 1)
+                if j == first + ROUND // 2 - 1:
+                    for nxt in following:
+                        quantise(nxt)
+            add_bias_on_vector(following)

@@ -109,12 +109,10 @@ def tile_timesformerlayer_pc_kernel(
         nc.sync.dma_start(
             out=w_words[:].bitcast(I32), in_=s_out_w_words.rearrange("g p n -> p g n").bitcast(I32)
         )
-        for quadrant in range(4):
+        for r in range(4):
             nc.sync.dma_start(
-                out=w_scales[32 * quadrant : 32 * quadrant + 4, :, :].bitcast(I32),
-                in_=s_out_w_scales[:, 4 * quadrant : 4 * quadrant + 4, :]
-                .rearrange("g r n -> r g n")
-                .bitcast(I32),
+                out=w_scales[r : P : 32, :, :].bitcast(I32),
+                in_=s_out_w_scales[:, r : 16 : 4, :].rearrange("g q n -> q g n").bitcast(I32),
             )
         residual = []
         for first in range(1, TILES, ROUND):
@@ -211,7 +209,10 @@ def tile_timesformerlayer_pc_kernel(
                 nc.vector.tensor_tensor(
                     out=result[p][:, cols], in0=product[:], in1=result[p][:, cols], op=ADD
                 )
-            nc.sync.dma_start(out=rows_of_patch(out, p), in_=result[p][:])
+                if p == PATCHES - 1:
+                    nc.sync.dma_start(out=rows_of_patch(out, p)[:, :, cols], in_=result[p][:, cols])
+            if p < PATCHES - 1:
+                nc.sync.dma_start(out=rows_of_patch(out, p), in_=result[p][:])
 
         class_sums = keep.tile([P, P], F32, name="class_sums")
         class_result = keep.tile([P, P], F32, name="class_result")

from contextlib import ExitStack

import concourse.mybir as mybir

F32 = mybir.dt.float32
BF16 = mybir.dt.bfloat16
I32 = mybir.dt.int32
U32 = mybir.dt.uint32
U8 = mybir.dt.uint8
FP8X4 = mybir.dt.float8_e4m3fn_x4
FP4X4 = mybir.dt.float4_e2m1fn_x4
ADD = mybir.AluOpType.add
MULT = mybir.AluOpType.mult
IS_EQUAL = mybir.AluOpType.is_equal

P = 128
SAMPLES = 16
FRAMES = 8
PATCHES = 12
TILES = 1 + PATCHES
D = 1024
K_PASS = 4 * P
PASSES = D // K_PASS
PAIRS = 2
BANK = 512
HALVES = D // BANK
CHUNKS = D // P
CHUNKS_A_BANK = BANK // P
ROUND = 2
TURNED_BANKS = 2
PRODUCT_BANKS = 4
VECTOR_EVERY = 3

FLOPS = 2 * TILES * P * D * D


def identity_by_vector(nc, pool):
    block = 32
    ones = pool.tile([P, P], F32, name="ones")
    nc.vector.memset(ones[:], 1.0)
    column = pool.tile([P, P], F32, name="column", align_bytes=64)
    nc.vector.tensor_tensor_scan(
        out=column[:], data0=ones[:], data1=ones[:], initial=-1.0, op0=MULT, op1=ADD
    )
    turned = pool.tile([P, P], F32, name="column_turned", align_bytes=64)
    nc.vector.transpose(out=turned[:], in_=column[:])
    identity = pool.tile([P, P], F32, name="identity")
    for first in range(0, P, block):
        rows = slice(first, first + block)
        nc.vector.tensor_scalar(
            out=identity[rows, :],
            in0=column[rows, :],
            scalar1=turned[rows, first : first + 1],
            scalar2=None,
            op0=IS_EQUAL,
        )
    return identity


def tile_timesformerlayer_pc_kernel(
    tc, ctx_s, x_res, s_out_w_words, s_out_w_scales, s_out_b, out
):
    nc = tc.nc
    with ExitStack() as stack:
        keep = stack.enter_context(tc.tile_pool(name="keep", bufs=1))
        ring = stack.enter_context(tc.tile_pool(name="ring", bufs=2 * ROUND))
        turned_banks = stack.enter_context(tc.psum_pool(name="turned_banks", bufs=TURNED_BANKS))
        product_banks = stack.enter_context(tc.psum_pool(name="product_banks", bufs=PRODUCT_BANKS))
        bias_banks = stack.enter_context(tc.psum_pool(name="bias_banks", bufs=1))
        stack.enter_context(tc.manual_schedule())

        w_scales = keep.tile([P, PASSES, D], U8, name="w_scales", align_bytes=64)
        nc.vector.memset(w_scales[:].rearrange("p g n -> p (g n)").bitcast(I32), 0)
        bias_chunks = keep.tile([P, P], BF16, name="bias_chunks")
        nc.vector.memset(bias_chunks[:], 0.0)
        identity = identity_by_vector(nc, keep)
        identity_bf = keep.tile([P, P], BF16, name="identity_bf")
        nc.vector.tensor_copy(out=identity_bf[:], in_=identity[:])
        chunk_of_row = keep.tile([P, P], BF16, name="chunk_of_row")
        nc.vector.tensor_copy(
            out=chunk_of_row[:].rearrange("p (c b) -> p c b", b=SAMPLES),
            in_=identity_bf[:, 0:CHUNKS].unsqueeze(2).to_broadcast([P, CHUNKS, SAMPLES]),
        )

        nc.scalar.dma_start(
            out=bias_chunks[0:CHUNKS, :], in_=s_out_b.rearrange("(c n) -> c n", c=CHUNKS)
        )
        class_residual = keep.tile([P, P], BF16, name="class_residual")
        nc.scalar.dma_start(
            out=class_residual[:], in_=x_res[:, 0, :].rearrange("b (c n) -> c b n", c=CHUNKS)
        )

        tokens = []
        class_tokens = keep.tile([P, D], BF16, name="class_tokens")
        nc.sync.dma_start(out=class_tokens[:], in_=ctx_s[:, 0, :])
        tokens.append(class_tokens[:])

        def load_tokens(first):
            both = keep.tile([P, ROUND, D], BF16, name="tokens%d" % first)
            nc.sync.dma_start(out=both[:], in_=ctx_s[:, first : first + ROUND, :])
            for i in range(ROUND):
                tokens.append(both[:, i, :])

        def rows_of_patch(tensor, p):
            return tensor[:, 1 + p * FRAMES : 1 + (p + 1) * FRAMES, :]

        load_tokens(1)
        w_words = keep.tile([P, PASSES, 2 * D], U8, name="w_words", align_bytes=64)
        nc.sync.dma_start(
            out=w_words[:].bitcast(I32), in_=s_out_w_words.rearrange("g p n -> p g n").bitcast(I32)
        )
        for r in range(4):
            nc.sync.dma_start(
                out=w_scales[r : P : 32, :, :].bitcast(I32),
                in_=s_out_w_scales[:, r : 16 : 4, :].rearrange("g q n -> q g n").bitcast(I32),
            )
        residual = []
        for first in range(1, TILES, ROUND):
            if first + ROUND < TILES:
                load_tokens(first + ROUND)
            for p in range(first - 1, first - 1 + ROUND):
                rows = keep.tile([P, D], BF16, name="residual%d" % p)
                nc.sync.dma_start(out=rows[:], in_=rows_of_patch(x_res, p))
                residual.append(rows)
        bias_bank = []
        bias_sb = keep.tile([P, D], F32, name="bias_sb")
        result = [keep.tile([P, D], F32, name="result%d" % p) for p in range(PATCHES)]

        def spread_bias():
            for h in range(HALVES):
                bank = bias_banks.tile([P, BANK], F32, name="bias_bank%d" % h)
                for i in range(CHUNKS_A_BANK):
                    c = h * CHUNKS_A_BANK + i
                    nc.tensor.matmul(
                        out=bank[:, i * P : (i + 1) * P],
                        lhsT=identity_bf[:, c : c + 1].to_broadcast([P, P]),
                        rhs=bias_chunks[:],
                        start=True,
                        stop=True,
                    )
                nc.vector.tensor_copy(out=bias_sb[:, h * BANK : (h + 1) * BANK], in_=bank[:])
                bias_bank.append(bank)
            class_bias = product_banks.tile([P, BANK], F32, name="product")
            nc.tensor.matmul(
                out=class_bias[:, 0:P], lhsT=chunk_of_row[:], rhs=bias_chunks[:], start=True, stop=True
            )
            nc.vector.tensor_tensor(
                out=class_result[:], in0=class_bias[:, 0:P], in1=class_residual[:], op=ADD
            )

        def add_bias_on_gpsimd():
            for p in range(PATCHES):
                if p % VECTOR_EVERY != 0:
                    nc.gpsimd.tensor_tensor(out=result[p][:], in0=residual[p][:], in1=bias_sb[:], op=ADD)

        def add_bias_on_vector(tiles):
            for j in tiles:
                p = j - 1
                if p % VECTOR_EVERY == 0:
                    for h in range(HALVES):
                        cols = slice(h * BANK, (h + 1) * BANK)
                        nc.vector.tensor_tensor(
                            out=result[p][:, cols], in0=bias_bank[h][:], in1=residual[p][:, cols], op=ADD
                        )

        grouped = {}
        codes = {}
        code_scales = {}

        def regroup(j):
            words = tokens[j].bitcast(F32)
            turned = turned_banks.tile([P, PASSES, PAIRS, P], F32, name="turned")
            for g in range(PASSES):
                for u in range(PAIRS):
                    nc.tensor.transpose(
                        turned[:, g, u, :],
                        words[:, g * PAIRS * P + u : (g + 1) * PAIRS * P : PAIRS],
                        identity[:],
                    )
            grouped[j] = ring.tile([P, D], BF16, name="grouped", align_bytes=64)
            nc.scalar.copy(
                out=grouped[j][:].bitcast(F32).rearrange("p (g r u) -> p g r u", g=PASSES, u=PAIRS),
                in_=turned[:].rearrange("p g u r -> p g r u"),
            )

        def quantise(j):
            codes[j] = ring.tile([P, PASSES * P], U32, name="codes", align_bytes=64)
            code_scales[j] = ring.tile([P, PASSES * P], U8, name="code_scales", align_bytes=64)
            nc.vector.quantize_mx(
                out=codes[j][:].bitcast(FP8X4), scales=code_scales[j][:], in_=grouped[j][:]
            )

        def multiply_patch(p):
            j = 1 + p
            for h in range(HALVES):
                cols = slice(h * BANK, (h + 1) * BANK)
                product = product_banks.tile([P, BANK], F32, name="product")
                for g in range(PASSES):
                    toks = slice(g * P, (g + 1) * P)
                    nc.tensor.matmul_mx(
                        out=product[:],
                        lhsT=codes[j][:, toks].bitcast(FP8X4),
                        lhsT_scale=code_scales[j][:, toks],
                        rhs=w_words[:, g, 2 * h * BANK : 2 * (h + 1) * BANK].bitcast(FP4X4),
                        rhs_scale=w_scales[:, g, cols],
                        start=(g == 0),
                        stop=(g == PASSES - 1),
                    )
                nc.vector.tensor_tensor(
                    out=result[p][:, cols], in0=product[:], in1=result[p][:, cols], op=ADD
                )
                if p == PATCHES - 1:
                    nc.sync.dma_start(out=rows_of_patch(out, p)[:, :, cols], in_=result[p][:, cols])
            if p < PATCHES - 1:
                nc.sync.dma_start(out=rows_of_patch(out, p), in_=result[p][:])

        class_sums = keep.tile([P, P], F32, name="class_sums")
        class_result = keep.tile([P, P], F32, name="class_result")

        def multiply_class_tokens():
            for bank in range(CHUNKS // CHUNKS_A_BANK):
                product = product_banks.tile([P, BANK], F32, name="product")
                for i in range(CHUNKS_A_BANK):
                    c = bank * CHUNKS_A_BANK + i
                    for g in range(PASSES):
                        toks = slice(g * P, (g + 1) * P)
                        nc.tensor.matmul_mx(
                            out=product[:, i * P : (i + 1) * P],
                            lhsT=w_words[:, g, 2 * c * P : 2 * (c + 1) * P].bitcast(FP4X4),
                            lhsT_scale=w_scales[:, g, c * P : (c + 1) * P],
                            rhs=codes[0][:, toks].bitcast(FP8X4),
                            rhs_scale=code_scales[0][:, toks],
                            start=(g == 0),
                            stop=(g == PASSES - 1),
                        )
                width = CHUNKS_A_BANK * SAMPLES
                nc.vector.tensor_reduce(
                    out=class_sums[:, bank * width : (bank + 1) * width],
                    in_=product[:].rearrange("p (m t) -> p m t", t=FRAMES),
                    axis=mybir.AxisListType.X,
                    op=ADD,
                )

        def finish_class_tokens():
            rows = product_banks.tile([P, BANK], F32, name="product")
            nc.tensor.transpose(rows[:, 0:P], class_sums[:], identity[:])
            nc.vector.scalar_tensor_tensor(
                out=class_result[:],
                in0=rows[:, 0:P],
                scalar=1.0 / FRAMES,
                in1=class_result[:],
                op0=MULT,
                op1=ADD,
            )
            nc.sync.dma_start(
                out=out[:, 0, :].rearrange("b (c n) -> c b n", c=CHUNKS), in_=class_result[:]
            )

        regroup(0)
        quantise(0)
        for j in range(1, 1 + ROUND):
            regroup(j)
        spread_bias()
        add_bias_on_gpsimd()
        for j in range(1, 1 + ROUND):
            quantise(j)
        multiply_class_tokens()
        add_bias_on_vector(range(1, 1 + ROUND))
        for first in range(1, TILES, ROUND):
            following = range(first + ROUND, min(first + 2 * ROUND, TILES))
            for j in following:
                regroup(j)
            if first == 1:
                finish_class_tokens()
            for j in range(first, first + ROUND):
                multiply_patch(j - 1)
                if j == first + ROUND // 2 - 1:
                    for nxt in following:
                        quantise(nxt)
            add_bias_on_vector(following)
